import numpy as np
import ml_dtypes


def mxq(x, axis, fmt="e4m3"):
    dtype, down = {"e4m3": (ml_dtypes.float8_e4m3fn, 7), "e5m2": (ml_dtypes.float8_e5m2, 14)}[fmt]
    v = np.moveaxis(np.asarray(x, np.float32).astype(ml_dtypes.bfloat16).astype(np.float64), axis, -1)
    blocks = v.reshape(v.shape[:-1] + (-1, 32))
    amax = np.abs(blocks).max(-1, keepdims=True)
    byte = np.maximum(np.where(amax > 0, np.frexp(amax)[1] - 1 + 127, 0) - down, 1)
    scale = np.exp2(byte - 127.0)
    codes = (blocks / scale).astype(np.float32).astype(dtype).astype(np.float64)
    return np.moveaxis((codes * scale).reshape(v.shape), -1, axis)


WIDE = False


def mx_kscale(k):
    if not WIDE:
        return np.ones(k)
    levels = np.array([10, -10, 5, -5, 0])
    a = np.random.permutation(np.resize(levels, k // 512 * 4)).reshape(k // 512, 4)
    idx = np.arange(k)
    return np.exp2(a[idx // 512, idx % 128 // 32])


BF16 = ml_dtypes.bfloat16


def bf(x):
    return np.asarray(x, np.float32).astype(BF16)


def f64(x):
    return np.asarray(x).astype(np.float64)


E2M1 = np.array([0.0, 0.5, 1.0, 1.5, 2.0, 3.0, 4.0, 6.0, -0.0, -0.5, -1.0, -1.5, -2.0, -3.0, -4.0, -6.0])


def pack_weight(w, fmt):
    k, n = w.shape
    w = f64(bf(w)).reshape(k // 32, 32, n)
    amax = np.abs(w).max(1)
    if fmt == "e4m3":
        byte = np.frexp(amax)[1] - 1 + 127 - 7
    else:
        mant, ex = np.frexp(amax / 6.0)
        byte = np.where(mant > 0.5, ex, ex - 1) + 127
    byte = np.clip(np.where(amax > 0, byte, 1), 1, 254)
    scaled = (w * np.exp2(127.0 - byte)[:, None, :]).reshape(k, n).astype(np.float32)
    by_word = np.ascontiguousarray(scaled.reshape(k // 512, 128, 4, n).transpose(0, 1, 3, 2))
    if fmt == "e4m3":
        words = by_word.astype(ml_dtypes.float8_e4m3fn).view(np.uint8)
    else:
        c = by_word.astype(ml_dtypes.float4_e2m1fn).view(np.uint8) & 0xF
        words = c[..., 0::2] | (c[..., 1::2] << 4)
    return np.ascontiguousarray(words), np.ascontiguousarray(byte.astype(np.uint8).reshape(k // 512, 16, n))


def unpack_weight(words, scales, fmt):
    g, p, n, _ = words.shape
    if fmt == "e4m3":
        vals = np.ascontiguousarray(words).view(ml_dtypes.float8_e4m3fn).astype(np.float64)
    else:
        nib = np.empty((g, p, n, 4), np.uint8)
        nib[..., 0::2] = words & 0xF
        nib[..., 1::2] = words >> 4
        vals = E2M1[nib]
    vals = vals * np.repeat(np.exp2(scales.astype(np.float64) - 127.0), 8, axis=1)[..., None]
    return vals.transpose(0, 1, 3, 2).reshape(g * 512, n)


B, S, H, NH, NKV, HD = 2, 512, 2048, 16, 4, 128
EPS = 1e-6
FMT = "e4m3"


def rms_norm(x, w):
    var = np.mean(x * x, axis=-1, keepdims=True)
    return x * (1.0 / np.sqrt(var + EPS)) * w


def rotate_half(x):
    x1, x2 = np.split(x, 2, axis=-1)
    return np.concatenate([-x2, x1], axis=-1)


def setup_inputs():
    s = mx_kscale(H)
    inv_freq = 1.0 / (10000.0 ** (np.arange(0, HD, 2) / HD))
    freqs = np.arange(S)[:, None] * inv_freq[None, :]
    emb = np.concatenate([freqs, freqs], axis=-1)
    hidden_states = bf(np.random.standard_normal((B, S, H)) * s)
    wq = np.random.standard_normal((NH * HD, H)) / np.sqrt(H) / s[None, :]
    wk = np.random.standard_normal((NKV * HD, H)) / np.sqrt(H) / s[None, :]
    wq_words, wq_scales = pack_weight(np.ascontiguousarray(wq.T), FMT)
    wk_words, wk_scales = pack_weight(np.ascontiguousarray(wk.T), FMT)
    return {"hidden_states": hidden_states,
            "cos": bf(np.cos(emb)),
            "sin": bf(np.sin(emb)),
            "wq_words": wq_words,
            "wq_scales": wq_scales,
            "wk_words": wk_words,
            "wk_scales": wk_scales,
            "q_norm_w": bf(1.0 + 0.1 * np.random.standard_normal(HD)),
            "k_norm_w": bf(1.0 + 0.1 * np.random.standard_normal(HD)),
            "ssmax_scale": bf((1.0 + 0.2 * np.random.standard_normal((1, NH, 1, 1))) / np.log(S))}


def reference(hidden_states, cos, sin, wq_words, wq_scales, wk_words, wk_scales, q_norm_w, k_norm_w, ssmax_scale):
    xq = mxq(f64(hidden_states), 2, "e4m3")
    q = (xq @ unpack_weight(wq_words, wq_scales, FMT)).reshape(B, S, NH, HD)
    k = (xq @ unpack_weight(wk_words, wk_scales, FMT)).reshape(B, S, NKV, HD)
    q = rms_norm(q, f64(q_norm_w)).transpose(0, 2, 1, 3)
    k = rms_norm(k, f64(k_norm_w)).transpose(0, 2, 1, 3)
    c = f64(cos)[None, None]
    sn = f64(sin)[None, None]
    q = q * c + rotate_half(q) * sn
    k = k * c + rotate_half(k) * sn
    q = q * (f64(ssmax_scale) * np.log(S))
    return q, k

@@ -1,0 +1,262 @@
+import math
+from contextlib import ExitStack
+
+import concourse.mybir as mybir
+from concourse.masks import make_identity
+
+F32 = mybir.dt.float32
+BF16 = mybir.dt.bfloat16
+I32 = mybir.dt.int32
+U32 = mybir.dt.uint32
+U8 = mybir.dt.uint8
+FP8X4 = mybir.dt.float8_e4m3fn_x4
+ACT = mybir.ActivationFunctionType
+ALU = mybir.AluOpType
+
+BATCH, SEQ, HIDDEN = 2, 512, 2048
+HEAD_DIM, Q_HEADS, K_HEADS = 128, 16, 4
+HALF = HEAD_DIM // 2
+EPS = 1e-6
+
+P = 128
+K_PASS = 4 * P
+PASSES = HIDDEN // K_PASS
+TILES = SEQ // P
+BANK = 512
+BANK_HEADS = BANK // HEAD_DIM
+Q_CHUNKS = Q_HEADS // BANK_HEADS
+CHUNKS = Q_CHUNKS + K_HEADS // BANK_HEADS
+COLUMNS = CHUNKS * BANK
+STEPS = BATCH * CHUNKS * TILES
+PREP_AHEAD = 2
+
+FLOPS = 2 * BATCH * SEQ * HIDDEN * COLUMNS
+
+
+def place(step):
+    batch, rest = divmod(step, CHUNKS * TILES)
+    chunk, tile_j = divmod(rest, TILES)
+    return batch, chunk, tile_j
+
+
+def tile_first_used_at(step):
+    if step >= STEPS:
+        return None
+    batch, chunk, tile_j = place(step)
+    return batch * TILES + tile_j if chunk == 0 else None
+
+
+def tile_biboattention_pa_kernel(
+    tc, hidden_states, cos, sin, wq_words, wq_scales, wk_words, wk_scales,
+    q_norm_w, k_norm_w, ssmax_scale, out_0, out_1,
+):
+    nc = tc.nc
+    with ExitStack() as ctx:
+        const = ctx.enter_context(tc.tile_pool(name="const", bufs=1))
+        resident = ctx.enter_context(tc.tile_pool(name="resident", bufs=1))
+        stage = ctx.enter_context(tc.tile_pool(name="stage", bufs=2))
+        small = ctx.enter_context(tc.tile_pool(name="small", bufs=4))
+        work = ctx.enter_context(tc.tile_pool(name="work", bufs=3))
+        psum_t = ctx.enter_context(tc.psum_pool(name="psum_t", bufs=2))
+        psum_acc = ctx.enter_context(tc.psum_pool(name="psum_acc", bufs=6))
+
+        x_raw = resident.tile([P, BATCH * TILES, HIDDEN], BF16)
+        x_codes = resident.tile([P, BATCH * TILES, PASSES * P], U32, align_bytes=64)
+        x_planes = resident.tile([P, BATCH * TILES, PASSES * P], U8, align_bytes=64)
+        w_codes = resident.tile([P, PASSES, COLUMNS], U32, align_bytes=64)
+        w_planes = resident.tile([P, COLUMNS], U8, align_bytes=64)
+
+        cos_sb = const.tile([P, TILES, HEAD_DIM], BF16)
+        sin_sb = const.tile([P, TILES, HEAD_DIM], BF16)
+        vector_rows = const.tile([P, BANK], BF16)
+        ones = const.tile([P, P], BF16)
+        identity = const.tile([P, P], F32)
+        eps = const.tile([P, 1], F32)
+        table_set = const.tile([P, 1], F32)
+        head_gain = const.tile([P, Q_HEADS], F32)
+        q_table_lo = const.tile([P, TILES, 2, HALF], F32)
+        q_table_hi = const.tile([P, TILES, 2, HALF], F32)
+        k_table_lo = const.tile([P, TILES, 2, HALF], F32)
+        k_table_hi = const.tile([P, TILES, 2, HALF], F32)
+
+        nc.vector.memset(vector_rows[:], 0.0)
+        nc.vector.memset(w_planes[:].bitcast(I32), 0)
+        nc.vector.memset(ones[:], 1.0)
+        nc.vector.memset(eps[:], EPS)
+        make_identity(nc, identity[:])
+        nc.scalar.activation(out=table_set[:], in_=eps[:], func=ACT.Sqrt)
+
+        x_view = hidden_states.rearrange("b (p j) k -> b j p k", j=TILES)
+        wq_view = wq_words.rearrange("g p n t -> p g (n t)").bitcast(I32)
+        wk_view = wk_words.rearrange("g p n t -> p g (n t)").bitcast(I32)
+
+        def load_x(t):
+            nc.sync.dma_start(out=x_raw[:, t, :], in_=x_view[t // TILES, t % TILES])
+
+        def load_w_scales(scales, first, width):
+            for quadrant in range(4):
+                nc.sync.dma_start(
+                    out=w_planes[32 * quadrant : 32 * quadrant + 16, first : first + width].bitcast(I32),
+                    in_=scales[:, 4 * quadrant : 4 * quadrant + 4, :].bitcast(I32),
+                )
+
+        def load_w(chunk):
+            columns = slice(chunk * BANK, (chunk + 1) * BANK)
+            if chunk == 0:
+                load_w_scales(wq_scales, 0, Q_CHUNKS * BANK)
+            if chunk == Q_CHUNKS:
+                load_w_scales(wk_scales, Q_CHUNKS * BANK, BANK)
+            source = wq_view[:, :, columns] if chunk < Q_CHUNKS else wk_view
+            nc.sync.dma_start(out=w_codes[:, :, columns].bitcast(I32), in_=source)
+
+        nc.sync.dma_start(out=cos_sb[:], in_=cos.rearrange("(p j) d -> p j d", j=TILES))
+        nc.sync.dma_start(out=sin_sb[:], in_=sin.rearrange("(p j) d -> p j d", j=TILES))
+        nc.sync.dma_start(out=vector_rows[0:1, 0:HEAD_DIM], in_=q_norm_w.rearrange("(o d) -> o d", o=1))
+        nc.sync.dma_start(out=vector_rows[0:1, HEAD_DIM : 2 * HEAD_DIM], in_=k_norm_w.rearrange("(o d) -> o d", o=1))
+        nc.sync.dma_start(
+            out=vector_rows[0:1, 2 * HEAD_DIM : 2 * HEAD_DIM + Q_HEADS],
+            in_=ssmax_scale.rearrange("a h b c -> a (h b c)"),
+        )
+        for t in range(PREP_AHEAD):
+            load_x(t)
+        for step in range(STEPS):
+            batch, chunk, tile_j = place(step)
+            if batch == 0 and tile_j == 0:
+                load_w(chunk)
+            if tile_first_used_at(step + PREP_AHEAD) is not None:
+                load_x(tile_first_used_at(step + PREP_AHEAD))
+
+        def transpose_x(t):
+            x_words = x_raw[:, t, :].bitcast(F32)
+            banks = []
+            for first_pass in range(0, PASSES, 2):
+                flipped = psum_t.tile([P, 2, 2, P], F32)
+                for g in range(2):
+                    for u in range(2):
+                        first_word = (K_PASS // 2) * (first_pass + g)
+                        nc.tensor.transpose(
+                            out=flipped[:, g, u, :],
+                            in_=x_words[:, first_word + u : first_word + K_PASS // 2 : 2],
+                            identity=identity[:],
+                        )
+                banks.append(flipped)
+            return banks
+
+        def regroup_x(banks):
+            grouped = stage.tile([P, PASSES * P * 4], BF16, align_bytes=64)
+            grouped_words = grouped[:].bitcast(F32).rearrange("p (g r u) -> p g r u", g=PASSES, u=2)
+            for i, flipped in enumerate(banks):
+                nc.scalar.copy(
+                    out=grouped_words[:, 2 * i : 2 * i + 2, :, :],
+                    in_=flipped[:].rearrange("p g u r -> p g r u"),
+                )
+            return grouped
+
+        def quantise_x(t, grouped):
+            nc.vector.quantize_mx(
+                out=x_codes[:, t, :].bitcast(FP8X4), scales=x_planes[:, t, :], in_=grouped[:]
+            )
+
+        def project(t, chunk):
+            acc = psum_acc.tile([P, BANK], F32, tag="acc")
+            columns = slice(chunk * BANK, (chunk + 1) * BANK)
+            for g in range(PASSES):
+                tokens = slice(g * P, (g + 1) * P)
+                nc.tensor.matmul_mx(
+                    out=acc[:],
+                    lhsT=x_codes[:, t, tokens].bitcast(FP8X4),
+                    lhsT_scale=x_planes[:, t, tokens],
+                    rhs=w_codes[:, g, columns].bitcast(FP8X4),
+                    rhs_scale=w_planes[4 * g : P, columns],
+                    start=(g == 0),
+                    stop=(g == PASSES - 1),
+                )
+            return acc
+
+        def row_factors(acc, chunk):
+            sum_sq = small.tile([P, BANK_HEADS], F32)
+            for h in range(BANK_HEADS):
+                squares = stage.tile([P, HEAD_DIM], F32)
+                nc.scalar.activation(
+                    out=squares[:], in_=acc[:, h * HEAD_DIM : (h + 1) * HEAD_DIM],
+                    func=ACT.Square, accum_out=sum_sq[:, h : h + 1],
+                )
+            rms = small.tile([P, BANK_HEADS], F32)
+            nc.scalar.activation(out=rms[:], in_=sum_sq[:], func=ACT.Sqrt, bias=eps[:], scale=1.0 / HEAD_DIM)
+            factor = small.tile([P, BANK_HEADS], F32)
+            nc.vector.reciprocal(out=factor[:], in_=rms[:])
+            if chunk < Q_CHUNKS:
+                heads = slice(chunk * BANK_HEADS, (chunk + 1) * BANK_HEADS)
+                nc.vector.tensor_mul(out=factor[:], in0=factor[:], in1=head_gain[:, heads])
+            return factor
+
+        def rotate(acc, factor, table_lo, table_hi, result):
+            from_lo = work.tile([P, BANK_HEADS, 2, HALF], F32)
+            from_hi = work.tile([P, BANK_HEADS, 2, HALF], F32)
+            for h in range(BANK_HEADS):
+                first = h * HEAD_DIM
+                for product, table, start in ((from_lo, table_lo, first), (from_hi, table_hi, first + HALF)):
+                    nc.vector.scalar_tensor_tensor(
+                        out=product[:, h, :, :],
+                        in0=acc[:, start : start + HALF].unsqueeze(1).to_broadcast([P, 2, HALF]),
+                        scalar=factor[:, h : h + 1],
+                        in1=table,
+                        op0=ALU.mult,
+                        op1=ALU.mult,
+                    )
+            nc.gpsimd.tensor_tensor(
+                out=result,
+                in0=from_lo[:].rearrange("p h s d -> p h (s d)"),
+                in1=from_hi[:].rearrange("p h s d -> p h (s d)"),
+                op=ALU.add,
+            )
+
+        for t in range(PREP_AHEAD):
+            quantise_x(t, regroup_x(transpose_x(t)))
+
+        spread = psum_acc.tile([P, BANK], F32, tag="acc")
+        nc.tensor.matmul(out=spread[:], lhsT=ones[:], rhs=vector_rows[:], start=True, stop=True)
+        for table_lo, table_hi, first in ((q_table_lo, q_table_hi, 0), (k_table_lo, k_table_hi, HEAD_DIM)):
+            w_lo = spread[:, first : first + HALF].unsqueeze(1).to_broadcast([P, TILES, HALF])
+            w_hi = spread[:, first + HALF : first + HEAD_DIM].unsqueeze(1).to_broadcast([P, TILES, HALF])
+            nc.vector.tensor_mul(out=table_lo[:, :, 0, :], in0=cos_sb[:, :, 0:HALF], in1=w_lo)
+            nc.vector.tensor_mul(out=table_lo[:, :, 1, :], in0=sin_sb[:, :, HALF:HEAD_DIM], in1=w_lo)
+            nc.vector.scalar_tensor_tensor(
+                out=table_hi[:, :, 0, :], in0=sin_sb[:, :, 0:HALF], scalar=-1.0, in1=w_hi,
+                op0=ALU.mult, op1=ALU.mult,
+            )
+            nc.vector.tensor_mul(out=table_hi[:, :, 1, :], in0=cos_sb[:, :, HALF:HEAD_DIM], in1=w_hi)
+        nc.vector.tensor_scalar_mul(
+            out=head_gain[:], in0=spread[:, 2 * HEAD_DIM : 2 * HEAD_DIM + Q_HEADS], scalar1=math.log(SEQ)
+        )
+
+        results = None
+        for step in range(STEPS):
+            batch, chunk, tile_j = place(step)
+            next_tile = tile_first_used_at(step + PREP_AHEAD)
+
+            acc = project(batch * TILES + tile_j, chunk)
+            if next_tile is not None:
+                banks = transpose_x(next_tile)
+            factor = row_factors(acc, chunk)
+            if next_tile is not None:
+                grouped = regroup_x(banks)
+
+            if tile_j == 0:
+                results = work.tile([P, BANK_HEADS, TILES, HEAD_DIM], F32)
+            if chunk < Q_CHUNKS:
+                rotate(acc, factor, q_table_lo[:, tile_j, :, :], q_table_hi[:, tile_j, :, :], results[:, :, tile_j, :])
+            else:
+                rotate(acc, factor, k_table_lo[:, tile_j, :, :], k_table_hi[:, tile_j, :, :], results[:, :, tile_j, :])
+            if next_tile is not None:
+                quantise_x(next_tile, grouped)
+
+            if tile_j == TILES - 1:
+                if chunk < Q_CHUNKS:
+                    target = out_0[batch, chunk * BANK_HEADS : (chunk + 1) * BANK_HEADS]
+                else:
+                    target = out_1[batch]
+                nc.sync.dma_start(
+                    out=target.rearrange("h (p j) d -> p h (j d)", j=TILES),
+                    in_=results[:].rearrange("p h j d -> p h (j d)"),
+                )

@@ -27,23 +27,8 @@ BANK_HEADS = BANK // HEAD_DIM
 Q_CHUNKS = Q_HEADS // BANK_HEADS
 CHUNKS = Q_CHUNKS + K_HEADS // BANK_HEADS
 COLUMNS = CHUNKS * BANK
-STEPS = BATCH * CHUNKS * TILES
-PREP_AHEAD = 2
 
 FLOPS = 2 * BATCH * SEQ * HIDDEN * COLUMNS
-
-
-def place(step):
-    batch, rest = divmod(step, CHUNKS * TILES)
-    chunk, tile_j = divmod(rest, TILES)
-    return batch, chunk, tile_j
-
-
-def tile_first_used_at(step):
-    if step >= STEPS:
-        return None
-    batch, chunk, tile_j = place(step)
-    return batch * TILES + tile_j if chunk == 0 else None
 
 
 def tile_biboattention_pa_kernel(
@@ -59,6 +44,7 @@ def tile_biboattention_pa_kernel(
         work = ctx.enter_context(tc.tile_pool(name="work", bufs=3))
         psum_t = ctx.enter_context(tc.psum_pool(name="psum_t", bufs=2))
         psum_acc = ctx.enter_context(tc.psum_pool(name="psum_acc", bufs=6))
+        ctx.enter_context(tc.manual_schedule())
 
         x_raw = resident.tile([P, BATCH * TILES, HIDDEN], BF16)
         x_codes = resident.tile([P, BATCH * TILES, PASSES * P], U32, align_bytes=64)
@@ -74,17 +60,15 @@ def tile_biboattention_pa_kernel(
         eps = const.tile([P, 1], F32)
         table_set = const.tile([P, 1], F32)
         head_gain = const.tile([P, Q_HEADS], F32)
-        q_table_lo = const.tile([P, TILES, 2, HALF], F32)
-        q_table_hi = const.tile([P, TILES, 2, HALF], F32)
-        k_table_lo = const.tile([P, TILES, 2, HALF], F32)
-        k_table_hi = const.tile([P, TILES, 2, HALF], F32)
+        q_table = const.tile([P, TILES, 2, 2, HALF], F32)
+        k_table = const.tile([P, TILES, 2, 2, HALF], F32)
 
         nc.vector.memset(vector_rows[:], 0.0)
         nc.vector.memset(w_planes[:].bitcast(I32), 0)
         nc.vector.memset(ones[:], 1.0)
         nc.vector.memset(eps[:], EPS)
         make_identity(nc, identity[:])
-        nc.scalar.activation(out=table_set[:], in_=eps[:], func=ACT.Sqrt)
+        nc.scalar.activation(out=table_set[:], in_=eps[:], func=ACT.Abs_reciprocal_sqrt)
 
         x_view = hidden_states.rearrange("b (p j) k -> b j p k", j=TILES)
         wq_view = wq_words.rearrange("g p n t -> p g (n t)").bitcast(I32)
@@ -117,14 +101,12 @@ def tile_biboattention_pa_kernel(
             out=vector_rows[0:1, 2 * HEAD_DIM : 2 * HEAD_DIM + Q_HEADS],
             in_=ssmax_scale.rearrange("a h b c -> a (h b c)"),
         )
-        for t in range(PREP_AHEAD):
+        for t in range(TILES):
             load_x(t)
-        for step in range(STEPS):
-            batch, chunk, tile_j = place(step)
-            if batch == 0 and tile_j == 0:
-                load_w(chunk)
-            if tile_first_used_at(step + PREP_AHEAD) is not None:
-                load_x(tile_first_used_at(step + PREP_AHEAD))
+        for chunk in range(CHUNKS):
+            load_w(chunk)
+            if chunk < TILES:
+                load_x(TILES + chunk)
 
         def transpose_x(t):
             x_words = x_raw[:, t, :].bitcast(F32)
@@ -181,77 +163,74 @@ def tile_biboattention_pa_kernel(
                     out=squares[:], in_=acc[:, h * HEAD_DIM : (h + 1) * HEAD_DIM],
                     func=ACT.Square, accum_out=sum_sq[:, h : h + 1],
                 )
-            rms = small.tile([P, BANK_HEADS], F32)
-            nc.scalar.activation(out=rms[:], in_=sum_sq[:], func=ACT.Sqrt, bias=eps[:], scale=1.0 / HEAD_DIM)
+            inverse_rms = small.tile([P, BANK_HEADS], F32)
+            nc.scalar.activation(
+                out=inverse_rms[:], in_=sum_sq[:], func=ACT.Abs_reciprocal_sqrt, bias=eps[:], scale=1.0 / HEAD_DIM
+            )
+            if chunk == Q_CHUNKS:
+                return inverse_rms
             factor = small.tile([P, BANK_HEADS], F32)
-            nc.vector.reciprocal(out=factor[:], in_=rms[:])
-            if chunk < Q_CHUNKS:
-                heads = slice(chunk * BANK_HEADS, (chunk + 1) * BANK_HEADS)
-                nc.vector.tensor_mul(out=factor[:], in0=factor[:], in1=head_gain[:, heads])
+            heads = slice(chunk * BANK_HEADS, (chunk + 1) * BANK_HEADS)
+            nc.vector.tensor_mul(out=factor[:], in0=inverse_rms[:], in1=head_gain[:, heads])
             return factor
 
-        def rotate(acc, factor, table_lo, table_hi, result):
-            from_lo = work.tile([P, BANK_HEADS, 2, HALF], F32)
-            from_hi = work.tile([P, BANK_HEADS, 2, HALF], F32)
+        def rotate(acc, factor, table, result):
+            products = work.tile([P, BANK_HEADS, 2, 2, HALF], F32)
             for h in range(BANK_HEADS):
-                first = h * HEAD_DIM
-                for product, table, start in ((from_lo, table_lo, first), (from_hi, table_hi, first + HALF)):
-                    nc.vector.scalar_tensor_tensor(
-                        out=product[:, h, :, :],
-                        in0=acc[:, start : start + HALF].unsqueeze(1).to_broadcast([P, 2, HALF]),
-                        scalar=factor[:, h : h + 1],
-                        in1=table,
-                        op0=ALU.mult,
-                        op1=ALU.mult,
-                    )
+                nc.vector.scalar_tensor_tensor(
+                    out=products[:, h, :, :, :].rearrange("p s f d -> p s (f d)"),
+                    in0=acc[:, h * HEAD_DIM : (h + 1) * HEAD_DIM].unsqueeze(1).to_broadcast([P, 2, HEAD_DIM]),
+                    scalar=factor[:, h : h + 1],
+                    in1=table.rearrange("p s f d -> p s (f d)"),
+                    op0=ALU.mult,
+                    op1=ALU.mult,
+                )
             nc.gpsimd.tensor_tensor(
-                out=result,
-                in0=from_lo[:].rearrange("p h s d -> p h (s d)"),
-                in1=from_hi[:].rearrange("p h s d -> p h (s d)"),
+                out=result.rearrange("p h (s d) -> p h s d", s=2),
+                in0=products[:, :, :, 0, :],
+                in1=products[:, :, :, 1, :],
                 op=ALU.add,
             )
 
-        for t in range(PREP_AHEAD):
-            quantise_x(t, regroup_x(transpose_x(t)))
+        quantise_x(0, regroup_x(transpose_x(0)))
 
         spread = psum_acc.tile([P, BANK], F32, tag="acc")
         nc.tensor.matmul(out=spread[:], lhsT=ones[:], rhs=vector_rows[:], start=True, stop=True)
-        for table_lo, table_hi, first in ((q_table_lo, q_table_hi, 0), (k_table_lo, k_table_hi, HEAD_DIM)):
+        for table, first in ((q_table, 0), (k_table, HEAD_DIM)):
             w_lo = spread[:, first : first + HALF].unsqueeze(1).to_broadcast([P, TILES, HALF])
             w_hi = spread[:, first + HALF : first + HEAD_DIM].unsqueeze(1).to_broadcast([P, TILES, HALF])
-            nc.vector.tensor_mul(out=table_lo[:, :, 0, :], in0=cos_sb[:, :, 0:HALF], in1=w_lo)
-            nc.vector.tensor_mul(out=table_lo[:, :, 1, :], in0=sin_sb[:, :, HALF:HEAD_DIM], in1=w_lo)
+            nc.vector.tensor_mul(out=table[:, :, 0, 0, :], in0=cos_sb[:, :, 0:HALF], in1=w_lo)
             nc.vector.scalar_tensor_tensor(
-                out=table_hi[:, :, 0, :], in0=sin_sb[:, :, 0:HALF], scalar=-1.0, in1=w_hi,
+                out=table[:, :, 0, 1, :], in0=sin_sb[:, :, 0:HALF], scalar=-1.0, in1=w_hi,
                 op0=ALU.mult, op1=ALU.mult,
             )
-            nc.vector.tensor_mul(out=table_hi[:, :, 1, :], in0=cos_sb[:, :, HALF:HEAD_DIM], in1=w_hi)
+            nc.vector.tensor_mul(out=table[:, :, 1, 0, :], in0=sin_sb[:, :, HALF:HEAD_DIM], in1=w_lo)
+            nc.vector.tensor_mul(out=table[:, :, 1, 1, :], in0=cos_sb[:, :, HALF:HEAD_DIM], in1=w_hi)
         nc.vector.tensor_scalar_mul(
             out=head_gain[:], in0=spread[:, 2 * HEAD_DIM : 2 * HEAD_DIM + Q_HEADS], scalar1=math.log(SEQ)
         )
 
-        results = None
-        for step in range(STEPS):
-            batch, chunk, tile_j = place(step)
-            next_tile = tile_first_used_at(step + PREP_AHEAD)
+        for t in range(1, TILES):
+            quantise_x(t, regroup_x(transpose_x(t)))
 
-            acc = project(batch * TILES + tile_j, chunk)
-            if next_tile is not None:
-                banks = transpose_x(next_tile)
-            factor = row_factors(acc, chunk)
-            if next_tile is not None:
-                grouped = regroup_x(banks)
-
-            if tile_j == 0:
+        for batch in range(BATCH):
+            for chunk in range(CHUNKS):
                 results = work.tile([P, BANK_HEADS, TILES, HEAD_DIM], F32)
-            if chunk < Q_CHUNKS:
-                rotate(acc, factor, q_table_lo[:, tile_j, :, :], q_table_hi[:, tile_j, :, :], results[:, :, tile_j, :])
-            else:
-                rotate(acc, factor, k_table_lo[:, tile_j, :, :], k_table_hi[:, tile_j, :, :], results[:, :, tile_j, :])
-            if next_tile is not None:
-                quantise_x(next_tile, grouped)
+                table = q_table if chunk < Q_CHUNKS else k_table
+                for tile_j in range(TILES):
+                    prepare = tile_j == 0 and chunk < TILES and batch + 1 < BATCH
+                    next_tile = (batch + 1) * TILES + chunk
 
-            if tile_j == TILES - 1:
+                    acc = project(batch * TILES + tile_j, chunk)
+                    if prepare:
+                        banks = transpose_x(next_tile)
+                    factor = row_factors(acc, chunk)
+                    if prepare:
+                        grouped = regroup_x(banks)
+                    rotate(acc, factor, table[:, tile_j, :, :, :], results[:, :, tile_j, :])
+                    if prepare:
+                        quantise_x(next_tile, grouped)
+
                 if chunk < Q_CHUNKS:
                     target = out_0[batch, chunk * BANK_HEADS : (chunk + 1) * BANK_HEADS]
                 else:

@@ -27,6 +27,7 @@ BANK_HEADS = BANK // HEAD_DIM
 Q_CHUNKS = Q_HEADS // BANK_HEADS
 CHUNKS = Q_CHUNKS + K_HEADS // BANK_HEADS
 COLUMNS = CHUNKS * BANK
+UP_FRONT = 3
 
 FLOPS = 2 * BATCH * SEQ * HIDDEN * COLUMNS
 
@@ -101,12 +102,12 @@ def tile_biboattention_pa_kernel(
             out=vector_rows[0:1, 2 * HEAD_DIM : 2 * HEAD_DIM + Q_HEADS],
             in_=ssmax_scale.rearrange("a h b c -> a (h b c)"),
         )
-        for t in range(TILES):
+        for t in range(UP_FRONT):
             load_x(t)
         for chunk in range(CHUNKS):
             load_w(chunk)
-            if chunk < TILES:
-                load_x(TILES + chunk)
+            if UP_FRONT + chunk < BATCH * TILES:
+                load_x(UP_FRONT + chunk)
 
         def transpose_x(t):
             x_words = x_raw[:, t, :].bitcast(F32)
@@ -174,8 +175,7 @@ def tile_biboattention_pa_kernel(
             nc.vector.tensor_mul(out=factor[:], in0=inverse_rms[:], in1=head_gain[:, heads])
             return factor
 
-        def rotate(acc, factor, table, result):
-            products = work.tile([P, BANK_HEADS, 2, 2, HALF], F32)
+        def multiply(acc, factor, table, products):
             for h in range(BANK_HEADS):
                 nc.vector.scalar_tensor_tensor(
                     out=products[:, h, :, :, :].rearrange("p s f d -> p s (f d)"),
@@ -185,14 +185,6 @@ def tile_biboattention_pa_kernel(
                     op0=ALU.mult,
                     op1=ALU.mult,
                 )
-            nc.gpsimd.tensor_tensor(
-                out=result.rearrange("p h (s d) -> p h s d", s=2),
-                in0=products[:, :, :, 0, :],
-                in1=products[:, :, :, 1, :],
-                op=ALU.add,
-            )
-
-        quantise_x(0, regroup_x(transpose_x(0)))
 
         spread = psum_acc.tile([P, BANK], F32, tag="acc")
         nc.tensor.matmul(out=spread[:], lhsT=ones[:], rhs=vector_rows[:], start=True, stop=True)
@@ -210,16 +202,21 @@ def tile_biboattention_pa_kernel(
             out=head_gain[:], in0=spread[:, 2 * HEAD_DIM : 2 * HEAD_DIM + Q_HEADS], scalar1=math.log(SEQ)
         )
 
-        for t in range(1, TILES):
+        for t in range(UP_FRONT):
             quantise_x(t, regroup_x(transpose_x(t)))
 
         for batch in range(BATCH):
             for chunk in range(CHUNKS):
-                results = work.tile([P, BANK_HEADS, TILES, HEAD_DIM], F32)
                 table = q_table if chunk < Q_CHUNKS else k_table
+                if chunk < Q_CHUNKS:
+                    target = out_0[batch, chunk * BANK_HEADS : (chunk + 1) * BANK_HEADS]
+                else:
+                    target = out_1[batch]
+                target = target.rearrange("h (p j) d -> p h j d", j=TILES)
+
                 for tile_j in range(TILES):
-                    prepare = tile_j == 0 and chunk < TILES and batch + 1 < BATCH
-                    next_tile = (batch + 1) * TILES + chunk
+                    next_tile = UP_FRONT + batch * CHUNKS + chunk
+                    prepare = tile_j == 0 and next_tile < BATCH * TILES
 
                     acc = project(batch * TILES + tile_j, chunk)
                     if prepare:
@@ -227,15 +224,20 @@ def tile_biboattention_pa_kernel(
                     factor = row_factors(acc, chunk)
                     if prepare:
                         grouped = regroup_x(banks)
-                    rotate(acc, factor, table[:, tile_j, :, :, :], results[:, :, tile_j, :])
+
+                    if tile_j % 2 == 0:
+                        products = work.tile([P, BANK_HEADS, 2, 2, 2, HALF], F32)
+                        results = work.tile([P, BANK_HEADS, 2, HEAD_DIM], F32)
+                    multiply(acc, factor, table[:, tile_j, :, :, :], products[:, :, tile_j % 2, :, :, :])
                     if prepare:
                         quantise_x(next_tile, grouped)
 
-                if chunk < Q_CHUNKS:
-                    target = out_0[batch, chunk * BANK_HEADS : (chunk + 1) * BANK_HEADS]
-                else:
-                    target = out_1[batch]
-                nc.sync.dma_start(
-                    out=target.rearrange("h (p j) d -> p h (j d)", j=TILES),
-                    in_=results[:].rearrange("p h j d -> p h (j d)"),
-                )
+                    if tile_j % 2 == 1:
+                        halves = products[:].rearrange("p h j s f d -> p (h j s) f d")
+                        nc.gpsimd.tensor_tensor(
+                            out=results[:].rearrange("p h j (s d) -> p (h j s) d", s=2),
+                            in0=halves[:, :, 0, :],
+                            in1=halves[:, :, 1, :],
+                            op=ALU.add,
+                        )
+                        nc.sync.dma_start(out=target[:, :, tile_j - 1 : tile_j + 1, :], in_=results[:])

@@ -27,7 +27,6 @@ BANK_HEADS = BANK // HEAD_DIM
 Q_CHUNKS = Q_HEADS // BANK_HEADS
 CHUNKS = Q_CHUNKS + K_HEADS // BANK_HEADS
 COLUMNS = CHUNKS * BANK
-UP_FRONT = 3
 
 FLOPS = 2 * BATCH * SEQ * HIDDEN * COLUMNS
 
@@ -44,7 +43,8 @@ def tile_biboattention_pa_kernel(
         small = ctx.enter_context(tc.tile_pool(name="small", bufs=4))
         work = ctx.enter_context(tc.tile_pool(name="work", bufs=3))
         psum_t = ctx.enter_context(tc.psum_pool(name="psum_t", bufs=2))
-        psum_acc = ctx.enter_context(tc.psum_pool(name="psum_acc", bufs=6))
+        psum_acc = ctx.enter_context(tc.psum_pool(name="psum_acc", bufs=5))
+        psum_const = ctx.enter_context(tc.psum_pool(name="psum_const", bufs=1))
         ctx.enter_context(tc.manual_schedule())
 
         x_raw = resident.tile([P, BATCH * TILES, HIDDEN], BF16)
@@ -60,7 +60,6 @@ def tile_biboattention_pa_kernel(
         identity = const.tile([P, P], F32)
         eps = const.tile([P, 1], F32)
         table_set = const.tile([P, 1], F32)
-        head_gain = const.tile([P, Q_HEADS], F32)
         q_table = const.tile([P, TILES, 2, 2, HALF], F32)
         k_table = const.tile([P, TILES, 2, 2, HALF], F32)
 
@@ -102,12 +101,12 @@ def tile_biboattention_pa_kernel(
             out=vector_rows[0:1, 2 * HEAD_DIM : 2 * HEAD_DIM + Q_HEADS],
             in_=ssmax_scale.rearrange("a h b c -> a (h b c)"),
         )
-        for t in range(UP_FRONT):
+        for t in range(TILES):
             load_x(t)
         for chunk in range(CHUNKS):
             load_w(chunk)
-            if UP_FRONT + chunk < BATCH * TILES:
-                load_x(UP_FRONT + chunk)
+            if chunk < TILES:
+                load_x(TILES + chunk)
 
         def transpose_x(t):
             x_words = x_raw[:, t, :].bitcast(F32)
@@ -175,7 +174,8 @@ def tile_biboattention_pa_kernel(
             nc.vector.tensor_mul(out=factor[:], in0=inverse_rms[:], in1=head_gain[:, heads])
             return factor
 
-        def multiply(acc, factor, table, products):
+        def rotate(acc, factor, table, result):
+            products = work.tile([P, BANK_HEADS, 2, 2, HALF], F32)
             for h in range(BANK_HEADS):
                 nc.vector.scalar_tensor_tensor(
                     out=products[:, h, :, :, :].rearrange("p s f d -> p s (f d)"),
@@ -185,38 +185,42 @@ def tile_biboattention_pa_kernel(
                     op0=ALU.mult,
                     op1=ALU.mult,
                 )
+            nc.gpsimd.tensor_tensor(
+                out=result.rearrange("p h (s d) -> p h s d", s=2),
+                in0=products[:, :, :, 0, :],
+                in1=products[:, :, :, 1, :],
+                op=ALU.add,
+            )
 
-        spread = psum_acc.tile([P, BANK], F32, tag="acc")
+        quantise_x(0, regroup_x(transpose_x(0)))
+
+        spread = psum_const.tile([P, BANK], F32)
         nc.tensor.matmul(out=spread[:], lhsT=ones[:], rhs=vector_rows[:], start=True, stop=True)
-        for table, first in ((q_table, 0), (k_table, HEAD_DIM)):
+        head_gain = spread[:, 2 * HEAD_DIM : 2 * HEAD_DIM + Q_HEADS]
+        for table, first, constant in ((q_table, 0, math.log(SEQ)), (k_table, HEAD_DIM, 1.0)):
             w_lo = spread[:, first : first + HALF].unsqueeze(1).to_broadcast([P, TILES, HALF])
             w_hi = spread[:, first + HALF : first + HEAD_DIM].unsqueeze(1).to_broadcast([P, TILES, HALF])
-            nc.vector.tensor_mul(out=table[:, :, 0, 0, :], in0=cos_sb[:, :, 0:HALF], in1=w_lo)
-            nc.vector.scalar_tensor_tensor(
-                out=table[:, :, 0, 1, :], in0=sin_sb[:, :, 0:HALF], scalar=-1.0, in1=w_hi,
-                op0=ALU.mult, op1=ALU.mult,
-            )
-            nc.vector.tensor_mul(out=table[:, :, 1, 0, :], in0=sin_sb[:, :, HALF:HEAD_DIM], in1=w_lo)
-            nc.vector.tensor_mul(out=table[:, :, 1, 1, :], in0=cos_sb[:, :, HALF:HEAD_DIM], in1=w_hi)
-        nc.vector.tensor_scalar_mul(
-            out=head_gain[:], in0=spread[:, 2 * HEAD_DIM : 2 * HEAD_DIM + Q_HEADS], scalar1=math.log(SEQ)
-        )
+            for row, half, angle, sign, w_half in (
+                (0, 0, cos_sb[:, :, 0:HALF], 1.0, w_lo),
+                (0, 1, sin_sb[:, :, 0:HALF], -1.0, w_hi),
+                (1, 0, sin_sb[:, :, HALF:HEAD_DIM], 1.0, w_lo),
+                (1, 1, cos_sb[:, :, HALF:HEAD_DIM], 1.0, w_hi),
+            ):
+                nc.vector.scalar_tensor_tensor(
+                    out=table[:, :, row, half, :], in0=angle, scalar=sign * constant, in1=w_half,
+                    op0=ALU.mult, op1=ALU.mult,
+                )
 
-        for t in range(UP_FRONT):
+        for t in range(1, TILES):
             quantise_x(t, regroup_x(transpose_x(t)))
 
         for batch in range(BATCH):
             for chunk in range(CHUNKS):
+                results = work.tile([P, BANK_HEADS, TILES, HEAD_DIM], F32)
                 table = q_table if chunk < Q_CHUNKS else k_table
-                if chunk < Q_CHUNKS:
-                    target = out_0[batch, chunk * BANK_HEADS : (chunk + 1) * BANK_HEADS]
-                else:
-                    target = out_1[batch]
-                target = target.rearrange("h (p j) d -> p h j d", j=TILES)
-
                 for tile_j in range(TILES):
-                    next_tile = UP_FRONT + batch * CHUNKS + chunk
-                    prepare = tile_j == 0 and next_tile < BATCH * TILES
+                    prepare = tile_j == 0 and chunk < TILES and batch + 1 < BATCH
+                    next_tile = (batch + 1) * TILES + chunk
 
                     acc = project(batch * TILES + tile_j, chunk)
                     if prepare:
@@ -224,20 +228,15 @@ def tile_biboattention_pa_kernel(
                     factor = row_factors(acc, chunk)
                     if prepare:
                         grouped = regroup_x(banks)
-
-                    if tile_j % 2 == 0:
-                        products = work.tile([P, BANK_HEADS, 2, 2, 2, HALF], F32)
-                        results = work.tile([P, BANK_HEADS, 2, HEAD_DIM], F32)
-                    multiply(acc, factor, table[:, tile_j, :, :, :], products[:, :, tile_j % 2, :, :, :])
+                    rotate(acc, factor, table[:, tile_j, :, :, :], results[:, :, tile_j, :])
                     if prepare:
                         quantise_x(next_tile, grouped)
 
-                    if tile_j % 2 == 1:
-                        halves = products[:].rearrange("p h j s f d -> p (h j s) f d")
-                        nc.gpsimd.tensor_tensor(
-                            out=results[:].rearrange("p h j (s d) -> p (h j s) d", s=2),
-                            in0=halves[:, :, 0, :],
-                            in1=halves[:, :, 1, :],
-                            op=ALU.add,
-                        )
-                        nc.sync.dma_start(out=target[:, :, tile_j - 1 : tile_j + 1, :], in_=results[:])
+                if chunk < Q_CHUNKS:
+                    target = out_0[batch, chunk * BANK_HEADS : (chunk + 1) * BANK_HEADS]
+                else:
+                    target = out_1[batch]
+                nc.sync.dma_start(
+                    out=target.rearrange("h (p j) d -> p h (j d)", j=TILES),
+                    in_=results[:].rearrange("p h j d -> p h (j d)"),
+                )

@@ -174,8 +174,7 @@ def tile_biboattention_pa_kernel(
             nc.vector.tensor_mul(out=factor[:], in0=inverse_rms[:], in1=head_gain[:, heads])
             return factor
 
-        def rotate(acc, factor, table, result):
-            products = work.tile([P, BANK_HEADS, 2, 2, HALF], F32)
+        def multiply(acc, factor, table, products):
             for h in range(BANK_HEADS):
                 nc.vector.scalar_tensor_tensor(
                     out=products[:, h, :, :, :].rearrange("p s f d -> p s (f d)"),
@@ -185,12 +184,17 @@ def tile_biboattention_pa_kernel(
                     op0=ALU.mult,
                     op1=ALU.mult,
                 )
+
+        def add_and_store(products, target):
+            results = work.tile([P, BANK_HEADS, 2, HEAD_DIM], F32)
+            halves = products[:].rearrange("p h j s f d -> p (h j s) f d")
             nc.gpsimd.tensor_tensor(
-                out=result.rearrange("p h (s d) -> p h s d", s=2),
-                in0=products[:, :, :, 0, :],
-                in1=products[:, :, :, 1, :],
+                out=results[:].rearrange("p h j (s d) -> p (h j s) d", s=2),
+                in0=halves[:, :, 0, :],
+                in1=halves[:, :, 1, :],
                 op=ALU.add,
             )
+            nc.sync.dma_start(out=target, in_=results[:])
 
         quantise_x(0, regroup_x(transpose_x(0)))
 
@@ -214,29 +218,41 @@ def tile_biboattention_pa_kernel(
         for t in range(1, TILES):
             quantise_x(t, regroup_x(transpose_x(t)))
 
+        steps = []
         for batch in range(BATCH):
             for chunk in range(CHUNKS):
-                results = work.tile([P, BANK_HEADS, TILES, HEAD_DIM], F32)
-                table = q_table if chunk < Q_CHUNKS else k_table
                 for tile_j in range(TILES):
-                    prepare = tile_j == 0 and chunk < TILES and batch + 1 < BATCH
-                    next_tile = (batch + 1) * TILES + chunk
+                    steps.append((batch, chunk, tile_j))
 
-                    acc = project(batch * TILES + tile_j, chunk)
-                    if prepare:
-                        banks = transpose_x(next_tile)
-                    factor = row_factors(acc, chunk)
-                    if prepare:
-                        grouped = regroup_x(banks)
-                    rotate(acc, factor, table[:, tile_j, :, :, :], results[:, :, tile_j, :])
-                    if prepare:
-                        quantise_x(next_tile, grouped)
+        waiting = None
+        products = None
+        for step in steps + [None]:
+            prepare = False
+            if step is not None:
+                batch, chunk, tile_j = step
+                prepare = tile_j == 2 and chunk < TILES and batch + 1 < BATCH
+                next_tile = (batch + 1) * TILES + chunk
 
-                if chunk < Q_CHUNKS:
-                    target = out_0[batch, chunk * BANK_HEADS : (chunk + 1) * BANK_HEADS]
-                else:
-                    target = out_1[batch]
-                nc.sync.dma_start(
-                    out=target.rearrange("h (p j) d -> p h (j d)", j=TILES),
-                    in_=results[:].rearrange("p h j d -> p h (j d)"),
-                )
+                acc = project(batch * TILES + tile_j, chunk)
+                if prepare:
+                    banks = transpose_x(next_tile)
+                factor = row_factors(acc, chunk)
+                if prepare:
+                    grouped = regroup_x(banks)
+
+            if waiting is not None:
+                full_acc, its_factor, (batch, chunk, tile_j) = waiting
+                table = q_table if chunk < Q_CHUNKS else k_table
+                if tile_j % 2 == 0:
+                    products = work.tile([P, BANK_HEADS, 2, 2, 2, HALF], F32)
+                multiply(full_acc, its_factor, table[:, tile_j, :, :, :], products[:, :, tile_j % 2, :, :, :])
+                if prepare:
+                    quantise_x(next_tile, grouped)
+                if tile_j % 2 == 1:
+                    if chunk < Q_CHUNKS:
+                        target = out_0[batch, chunk * BANK_HEADS : (chunk + 1) * BANK_HEADS]
+                    else:
+                        target = out_1[batch]
+                    target = target.rearrange("h (p j) d -> p h j d", j=TILES)
+                    add_and_store(products, target[:, :, tile_j - 1 : tile_j + 1, :])
+            waiting = (acc, factor, step)

@@ -185,10 +185,10 @@ def tile_biboattention_pa_kernel(
                     op1=ALU.mult,
                 )
 
-        def add_and_store(products, target):
+        def add_and_store(engine, products, target):
             results = work.tile([P, BANK_HEADS, 2, HEAD_DIM], F32)
             halves = products[:].rearrange("p h j s f d -> p (h j s) f d")
-            nc.gpsimd.tensor_tensor(
+            engine.tensor_tensor(
                 out=results[:].rearrange("p h j (s d) -> p (h j s) d", s=2),
                 in0=halves[:, :, 0, :],
                 in1=halves[:, :, 1, :],
@@ -254,5 +254,6 @@ def tile_biboattention_pa_kernel(
                     else:
                         target = out_1[batch]
                     target = target.rearrange("h (p j) d -> p h j d", j=TILES)
-                    add_and_store(products, target[:, :, tile_j - 1 : tile_j + 1, :])
+                    adder = nc.vector if step is None else nc.gpsimd
+                    add_and_store(adder, products, target[:, :, tile_j - 1 : tile_j + 1, :])
             waiting = (acc, factor, step)

@@ -48,10 +48,10 @@ def tile_biboattention_pa_kernel(
         ctx.enter_context(tc.manual_schedule())
 
         x_raw = resident.tile([P, BATCH * TILES, HIDDEN], BF16)
-        x_codes = resident.tile([P, BATCH * TILES, PASSES * P], U32, align_bytes=64)
-        x_planes = resident.tile([P, BATCH * TILES, PASSES * P], U8, align_bytes=64)
-        w_codes = resident.tile([P, PASSES, COLUMNS], U32, align_bytes=64)
-        w_planes = resident.tile([P, COLUMNS], U8, align_bytes=64)
+        x_codes = resident.tile([P, BATCH * TILES, PASSES * P], U32, align_bytes=256)
+        x_planes = resident.tile([P, BATCH * TILES, PASSES * P], U8, align_bytes=256)
+        w_codes = resident.tile([P, PASSES, COLUMNS], U32, align_bytes=256)
+        w_planes = resident.tile([P, COLUMNS], U8, align_bytes=256)
 
         cos_sb = const.tile([P, TILES, HEAD_DIM], BF16)
         sin_sb = const.tile([P, TILES, HEAD_DIM], BF16)

@@ -41,6 +41,7 @@ def tile_biboattention_pa_kernel(
         resident = ctx.enter_context(tc.tile_pool(name="resident", bufs=1))
         stage = ctx.enter_context(tc.tile_pool(name="stage", bufs=2))
         small = ctx.enter_context(tc.tile_pool(name="small", bufs=4))
+        unread = ctx.enter_context(tc.tile_pool(name="unread", bufs=8))
         work = ctx.enter_context(tc.tile_pool(name="work", bufs=3))
         psum_t = ctx.enter_context(tc.psum_pool(name="psum_t", bufs=2))
         psum_acc = ctx.enter_context(tc.psum_pool(name="psum_acc", bufs=5))
@@ -158,7 +159,7 @@ def tile_biboattention_pa_kernel(
         def row_factors(acc, chunk):
             sum_sq = small.tile([P, BANK_HEADS], F32)
             for h in range(BANK_HEADS):
-                squares = stage.tile([P, HEAD_DIM], F32)
+                squares = unread.tile([P, HEAD_DIM], F32)
                 nc.scalar.activation(
                     out=squares[:], in_=acc[:, h * HEAD_DIM : (h + 1) * HEAD_DIM],
                     func=ACT.Square, accum_out=sum_sq[:, h : h + 1],

import math
from contextlib import ExitStack

import concourse.mybir as mybir
from concourse.masks import make_identity

F32 = mybir.dt.float32
BF16 = mybir.dt.bfloat16
I32 = mybir.dt.int32
U32 = mybir.dt.uint32
U8 = mybir.dt.uint8
FP8X4 = mybir.dt.float8_e4m3fn_x4
ACT = mybir.ActivationFunctionType
ALU = mybir.AluOpType

BATCH, SEQ, HIDDEN = 2, 512, 2048
HEAD_DIM, Q_HEADS, K_HEADS = 128, 16, 4
HALF = HEAD_DIM // 2
EPS = 1e-6

P = 128
K_PASS = 4 * P
PASSES = HIDDEN // K_PASS
TILES = SEQ // P
BANK = 512
BANK_HEADS = BANK // HEAD_DIM
Q_CHUNKS = Q_HEADS // BANK_HEADS
CHUNKS = Q_CHUNKS + K_HEADS // BANK_HEADS
COLUMNS = CHUNKS * BANK

FLOPS = 2 * BATCH * SEQ * HIDDEN * COLUMNS


def tile_biboattention_pa_kernel(
    tc, hidden_states, cos, sin, wq_words, wq_scales, wk_words, wk_scales,
    q_norm_w, k_norm_w, ssmax_scale, out_0, out_1,
):
    nc = tc.nc
    with ExitStack() as ctx:
        const = ctx.enter_context(tc.tile_pool(name="const", bufs=1))
        resident = ctx.enter_context(tc.tile_pool(name="resident", bufs=1))
        stage = ctx.enter_context(tc.tile_pool(name="stage", bufs=2))
        small = ctx.enter_context(tc.tile_pool(name="small", bufs=4))
        unread = ctx.enter_context(tc.tile_pool(name="unread", bufs=8))
        work = ctx.enter_context(tc.tile_pool(name="work", bufs=3))
        psum_t = ctx.enter_context(tc.psum_pool(name="psum_t", bufs=2))
        psum_acc = ctx.enter_context(tc.psum_pool(name="psum_acc", bufs=5))
        psum_const = ctx.enter_context(tc.psum_pool(name="psum_const", bufs=1))
        ctx.enter_context(tc.manual_schedule())

        x_raw = resident.tile([P, BATCH * TILES, HIDDEN], BF16)
        x_codes = resident.tile([P, BATCH * TILES, PASSES * P], U32, align_bytes=256)
        x_planes = resident.tile([P, BATCH * TILES, PASSES * P], U8, align_bytes=256)
        w_codes = resident.tile([P, PASSES, COLUMNS], U32, align_bytes=256)
        w_planes = resident.tile([P, COLUMNS], U8, align_bytes=256)

        cos_sb = const.tile([P, TILES, HEAD_DIM], BF16)
        sin_sb = const.tile([P, TILES, HEAD_DIM], BF16)
        vector_rows = const.tile([P, BANK], BF16)
        ones = const.tile([P, P], BF16)
        identity = const.tile([P, P], F32)
        eps = const.tile([P, 1], F32)
        table_set = const.tile([P, 1], F32)
        q_table = const.tile([P, TILES, 2, 2, HALF], F32)
        k_table = const.tile([P, TILES, 2, 2, HALF], F32)

        nc.vector.memset(vector_rows[:], 0.0)
        nc.vector.memset(w_planes[:].bitcast(I32), 0)
        nc.vector.memset(ones[:], 1.0)
        nc.vector.memset(eps[:], EPS)
        make_identity(nc, identity[:])
        nc.scalar.activation(out=table_set[:], in_=eps[:], func=ACT.Abs_reciprocal_sqrt)

        x_view = hidden_states.rearrange("b (p j) k -> b j p k", j=TILES)
        wq_view = wq_words.rearrange("g p n t -> p g (n t)").bitcast(I32)
        wk_view = wk_words.rearrange("g p n t -> p g (n t)").bitcast(I32)

        def load_x(t):
            nc.sync.dma_start(out=x_raw[:, t, :], in_=x_view[t // TILES, t % TILES])

        def load_w_scales(scales, first, width):
            for quadrant in range(4):
                nc.sync.dma_start(
                    out=w_planes[32 * quadrant : 32 * quadrant + 16, first : first + width].bitcast(I32),
                    in_=scales[:, 4 * quadrant : 4 * quadrant + 4, :].bitcast(I32),
                )

        def load_w(chunk):
            columns = slice(chunk * BANK, (chunk + 1) * BANK)
            if chunk == 0:
                load_w_scales(wq_scales, 0, Q_CHUNKS * BANK)
            if chunk == Q_CHUNKS:
                load_w_scales(wk_scales, Q_CHUNKS * BANK, BANK)
            source = wq_view[:, :, columns] if chunk < Q_CHUNKS else wk_view
            nc.sync.dma_start(out=w_codes[:, :, columns].bitcast(I32), in_=source)

        nc.sync.dma_start(out=cos_sb[:], in_=cos.rearrange("(p j) d -> p j d", j=TILES))
        nc.sync.dma_start(out=sin_sb[:], in_=sin.rearrange("(p j) d -> p j d", j=TILES))
        nc.sync.dma_start(out=vector_rows[0:1, 0:HEAD_DIM], in_=q_norm_w.rearrange("(o d) -> o d", o=1))
        nc.sync.dma_start(out=vector_rows[0:1, HEAD_DIM : 2 * HEAD_DIM], in_=k_norm_w.rearrange("(o d) -> o d", o=1))
        nc.sync.dma_start(
            out=vector_rows[0:1, 2 * HEAD_DIM : 2 * HEAD_DIM + Q_HEADS],
            in_=ssmax_scale.rearrange("a h b c -> a (h b c)"),
        )
        for t in range(TILES):
            load_x(t)
        for chunk in range(CHUNKS):
            load_w(chunk)
            if chunk < TILES:
                load_x(TILES + chunk)

        def transpose_x(t):
            x_words = x_raw[:, t, :].bitcast(F32)
            banks = []
            for first_pass in range(0, PASSES, 2):
                flipped = psum_t.tile([P, 2, 2, P], F32)
                for g in range(2):
                    for u in range(2):
                        first_word = (K_PASS // 2) * (first_pass + g)
                        nc.tensor.transpose(
                            out=flipped[:, g, u, :],
                            in_=x_words[:, first_word + u : first_word + K_PASS // 2 : 2],
                            identity=identity[:],
                        )
                banks.append(flipped)
            return banks

        def regroup_x(banks):
            grouped = stage.tile([P, PASSES * P * 4], BF16, align_bytes=64)
            grouped_words = grouped[:].bitcast(F32).rearrange("p (g r u) -> p g r u", g=PASSES, u=2)
            for i, flipped in enumerate(banks):
                nc.scalar.copy(
                    out=grouped_words[:, 2 * i : 2 * i + 2, :, :],
                    in_=flipped[:].rearrange("p g u r -> p g r u"),
                )
            return grouped

        def quantise_x(t, grouped):
            nc.vector.quantize_mx(
                out=x_codes[:, t, :].bitcast(FP8X4), scales=x_planes[:, t, :], in_=grouped[:]
            )

        def project(t, chunk):
            acc = psum_acc.tile([P, BANK], F32, tag="acc")
            columns = slice(chunk * BANK, (chunk + 1) * BANK)
            for g in range(PASSES):
                tokens = slice(g * P, (g + 1) * P)
                nc.tensor.matmul_mx(
                    out=acc[:],
                    lhsT=x_codes[:, t, tokens].bitcast(FP8X4),
                    lhsT_scale=x_planes[:, t, tokens],
                    rhs=w_codes[:, g, columns].bitcast(FP8X4),
                    rhs_scale=w_planes[4 * g : P, columns],
                    start=(g == 0),
                    stop=(g == PASSES - 1),
                )
            return acc

        def row_factors(acc, chunk):
            sum_sq = small.tile([P, BANK_HEADS], F32)
            for h in range(BANK_HEADS):
                squares = unread.tile([P, HEAD_DIM], F32)
                nc.scalar.activation(
                    out=squares[:], in_=acc[:, h * HEAD_DIM : (h + 1) * HEAD_DIM],
                    func=ACT.Square, accum_out=sum_sq[:, h : h + 1],
                )
            inverse_rms = small.tile([P, BANK_HEADS], F32)
            nc.scalar.activation(
                out=inverse_rms[:], in_=sum_sq[:], func=ACT.Abs_reciprocal_sqrt, bias=eps[:], scale=1.0 / HEAD_DIM
            )
            if chunk == Q_CHUNKS:
                return inverse_rms
            factor = small.tile([P, BANK_HEADS], F32)
            heads = slice(chunk * BANK_HEADS, (chunk + 1) * BANK_HEADS)
            nc.vector.tensor_mul(out=factor[:], in0=inverse_rms[:], in1=head_gain[:, heads])
            return factor

        def multiply(acc, factor, table, products):
            for h in range(BANK_HEADS):
                nc.vector.scalar_tensor_tensor(
                    out=products[:, h, :, :, :].rearrange("p s f d -> p s (f d)"),
                    in0=acc[:, h * HEAD_DIM : (h + 1) * HEAD_DIM].unsqueeze(1).to_broadcast([P, 2, HEAD_DIM]),
                    scalar=factor[:, h : h + 1],
                    in1=table.rearrange("p s f d -> p s (f d)"),
                    op0=ALU.mult,
                    op1=ALU.mult,
                )

        def add_and_store(engine, products, target):
            results = work.tile([P, BANK_HEADS, 2, HEAD_DIM], F32)
            halves = products[:].rearrange("p h j s f d -> p (h j s) f d")
            engine.tensor_tensor(
                out=results[:].rearrange("p h j (s d) -> p (h j s) d", s=2),
                in0=halves[:, :, 0, :],
                in1=halves[:, :, 1, :],
                op=ALU.add,
            )
            nc.sync.dma_start(out=target, in_=results[:])

        quantise_x(0, regroup_x(transpose_x(0)))

        spread = psum_const.tile([P, BANK], F32)
        nc.tensor.matmul(out=spread[:], lhsT=ones[:], rhs=vector_rows[:], start=True, stop=True)
        head_gain = spread[:, 2 * HEAD_DIM : 2 * HEAD_DIM + Q_HEADS]
        for table, first, constant in ((q_table, 0, math.log(SEQ)), (k_table, HEAD_DIM, 1.0)):
            w_lo = spread[:, first : first + HALF].unsqueeze(1).to_broadcast([P, TILES, HALF])
            w_hi = spread[:, first + HALF : first + HEAD_DIM].unsqueeze(1).to_broadcast([P, TILES, HALF])
            for row, half, angle, sign, w_half in (
                (0, 0, cos_sb[:, :, 0:HALF], 1.0, w_lo),
                (0, 1, sin_sb[:, :, 0:HALF], -1.0, w_hi),
                (1, 0, sin_sb[:, :, HALF:HEAD_DIM], 1.0, w_lo),
                (1, 1, cos_sb[:, :, HALF:HEAD_DIM], 1.0, w_hi),
            ):
                nc.vector.scalar_tensor_tensor(
                    out=table[:, :, row, half, :], in0=angle, scalar=sign * constant, in1=w_half,
                    op0=ALU.mult, op1=ALU.mult,
                )

        for t in range(1, TILES):
            quantise_x(t, regroup_x(transpose_x(t)))

        steps = []
        for batch in range(BATCH):
            for chunk in range(CHUNKS):
                for tile_j in range(TILES):
                    steps.append((batch, chunk, tile_j))

        waiting = None
        products = None
        for step in steps + [None]:
            prepare = False
            if step is not None:
                batch, chunk, tile_j = step
                prepare = tile_j == 2 and chunk < TILES and batch + 1 < BATCH
                next_tile = (batch + 1) * TILES + chunk

                acc = project(batch * TILES + tile_j, chunk)
                if prepare:
                    banks = transpose_x(next_tile)
                factor = row_factors(acc, chunk)
                if prepare:
                    grouped = regroup_x(banks)

            if waiting is not None:
                full_acc, its_factor, (batch, chunk, tile_j) = waiting
                table = q_table if chunk < Q_CHUNKS else k_table
                if tile_j % 2 == 0:
                    products = work.tile([P, BANK_HEADS, 2, 2, 2, HALF], F32)
                multiply(full_acc, its_factor, table[:, tile_j, :, :, :], products[:, :, tile_j % 2, :, :, :])
                if prepare:
                    quantise_x(next_tile, grouped)
                if tile_j % 2 == 1:
                    if chunk < Q_CHUNKS:
                        target = out_0[batch, chunk * BANK_HEADS : (chunk + 1) * BANK_HEADS]
                    else:
                        target = out_1[batch]
                    target = target.rearrange("h (p j) d -> p h j d", j=TILES)
                    adder = nc.vector if step is None else nc.gpsimd
                    add_and_store(adder, products, target[:, :, tile_j - 1 : tile_j + 1, :])
            waiting = (acc, factor, step)
